import numpy as np
import ml_dtypes


def mxq(x, axis, fmt="e4m3"):
    dtype, down = {"e4m3": (ml_dtypes.float8_e4m3fn, 7), "e5m2": (ml_dtypes.float8_e5m2, 14)}[fmt]
    v = np.moveaxis(np.asarray(x, np.float32).astype(ml_dtypes.bfloat16).astype(np.float64), axis, -1)
    blocks = v.reshape(v.shape[:-1] + (-1, 32))
    amax = np.abs(blocks).max(-1, keepdims=True)
    byte = np.maximum(np.where(amax > 0, np.frexp(amax)[1] - 1 + 127, 0) - down, 1)
    scale = np.exp2(byte - 127.0)
    codes = (blocks / scale).astype(np.float32).astype(dtype).astype(np.float64)
    return np.moveaxis((codes * scale).reshape(v.shape), -1, axis)


WIDE = False


def mx_kscale(k):
    if not WIDE:
        return np.ones(k)
    levels = np.array([20, -20, 10, -10, 0])
    a = np.random.permutation(np.resize(levels, k // 512 * 4)).reshape(k // 512, 4)
    idx = np.arange(k)
    return np.exp2(a[idx // 512, idx % 128 // 32])


BF16 = ml_dtypes.bfloat16


def bf(x):
    return np.asarray(x, np.float32).astype(BF16)


def f64(x):
    return np.asarray(x).astype(np.float64)


B, F, DOF, N_CLS = 1024, 64, 64, 1024
K = F * DOF


def setup_inputs():
    s = mx_kscale(B)
    c = float(s.max()) if s.max() > max(s.min(), 1.0) else 1.0
    far = np.repeat(s.reshape(B // 32, 32)[:, 0] == s.max(), 32) & (c > 1.0)
    lo, hi = -3.0 / c, 3.0
    pos = 0.5 + np.random.standard_normal((B, F)) / 6.0
    pos = np.where(far[:, None], 1.5 + 0.25 * pos, pos)
    xv = f64(bf(lo + (hi - lo) * pos))
    xv[xv == hi] = 2.5
    xv[xv == lo] = -2.5
    xv[(c > 1.0) & ((xv == 1.0) | (xv == 2.0))] += 2.0**-6
    w = np.random.standard_normal((N_CLS, K)) * 0.005
    g = np.random.standard_normal((B, N_CLS)) * np.exp2(np.random.randint(-12, 1, (B, 1))) * 0.25 * np.where(far, c, 1.0)[:, None]
    return {"x": bf(xv), "min_x": bf(np.array([lo])), "max_x": bf(np.array([hi])),
            "W": bf(w), "dof": DOF, "grad_out": bf(g)}


def _lagrange_embed(x, min_x, max_x, dof):
    b_, f_ = x.shape
    T = dof - 1
    h = 1.0 / T
    xn = ((x.reshape(-1, 1) - min_x) / (max_x - min_x)).reshape(-1)
    t = np.arange(T, dtype=np.float64)
    s = xn[:, None] / h
    lam0 = s - t
    lam1 = (t + 1.0) - s
    n2t = ((lam0 >= 0.0) & (lam1 >= 0.0)).astype(np.float64)
    z = np.zeros((xn.shape[0], 1), dtype=np.float64)
    mask = np.concatenate([n2t, z], axis=1) + np.concatenate([z, n2t], axis=1)
    w0 = n2t * lam0
    w1 = n2t * lam1
    shape_vals = np.concatenate([w1, z], axis=1) + np.concatenate([z, w0], axis=1)
    basis = shape_vals / np.maximum(mask, 1.0)
    emb = basis * (max_x - min_x) + min_x
    return emb.reshape(b_, f_ * dof)


def reference(x, min_x, max_x, W, dof, grad_out):
    emb = _lagrange_embed(f64(x), f64(min_x), f64(max_x), int(dof))
    return mxq(f64(grad_out), 0, "e5m2").T @ mxq(emb, 0, "e4m3")

@@ -1,0 +1,261 @@
+from contextlib import ExitStack
+
+import concourse.mybir as mybir
+
+F32 = mybir.dt.float32
+BF16 = mybir.dt.bfloat16
+U32 = mybir.dt.uint32
+U8 = mybir.dt.uint8
+E4X4 = mybir.dt.float8_e4m3fn_x4
+E5X4 = mybir.dt.float8_e5m2_x4
+ALU = mybir.AluOpType
+ACT = mybir.ActivationFunctionType
+
+P = 128
+B, F, DOF, N_CLS = 1024, 64, 64, 1024
+K = F * DOF
+FLOPS = 2 * B * N_CLS * K
+BYTES = 4 * N_CLS * K + 2 * B * N_CLS + 2 * B * F + 4
+
+GROUPS = ((0,), (1,), (2, 3), (4, 5, 6, 7))
+VECTOR_BANKS = {0: (7,), 1: (7,), 2: (7,), 3: (7,), 4: (7,), 5: (7,), 6: (7,), 7: (1, 3, 5, 7)}
+
+
+def tile_lagrangenet_kernel(tc, x, min_x, max_x, W, dof, grad_out, out):
+    nc = tc.nc
+    assert dof == DOF
+    with ExitStack() as ctx:
+        keep = ctx.enter_context(tc.tile_pool(name="keep", bufs=1))
+        embp = ctx.enter_context(tc.tile_pool(name="embp", bufs=3))
+        codep = ctx.enter_context(tc.tile_pool(name="codep", bufs=4))
+        stagep = ctx.enter_context(tc.tile_pool(name="stagep", bufs=12))
+        psum = ctx.enter_context(tc.psum_pool(name="acc", bufs=8))
+
+        m_bf = keep.tile([P, 1], BF16, name="m_bf")
+        big_bf = keep.tile([P, 1], BF16, name="big_bf")
+        x_sb = keep.tile([P, 2, 4, F], BF16, name="x_sb")
+        g_raw = keep.tile([P, 2, 4, N_CLS], BF16, name="g_raw")
+        nc.sync.dma_start(out=m_bf[:], in_=min_x.partition_broadcast(P))
+        nc.sync.dma_start(out=big_bf[:], in_=max_x.partition_broadcast(P))
+        nc.sync.dma_start(out=x_sb[:], in_=x.rearrange("(g p t) f -> p g t f", g=2, p=P, t=4))
+        for g in range(2):
+            nc.sync.dma_start(
+                out=g_raw[:, g],
+                in_=grad_out[g * 512 : (g + 1) * 512, :].rearrange("(p j) n -> p j n", j=4),
+            )
+
+        tab0 = keep.tile([P, 20], F32, name="tab0")
+        consts = [-(8.0 * a + 3.5) for a in range(8)] + [-31.5, -16.0, -8.0, 8.0] + [-(c + 0.5) for c in range(8)]
+        for j, v in enumerate(consts):
+            nc.vector.memset(tab0[:, j : j + 1], v)
+        warm = keep.tile([P, 1], F32, name="warm")
+        nc.scalar.activation(out=warm[:], in_=tab0[:, 0:1], func=ACT.Abs)
+
+        big_f = keep.tile([P, 1], F32, name="big_f")
+        rng = keep.tile([P, 1], F32, name="rng")
+        rinv = keep.tile([P, 1], F32, name="rinv")
+        c63 = keep.tile([P, 1], F32, name="c63")
+        mc = keep.tile([P, 1], F32, name="mc")
+        tabr = keep.tile([P, 9], F32, name="tabr")
+        neg_r = keep.tile([P, 1], F32, name="neg_r")
+        neg_2r = keep.tile([P, 1], F32, name="neg_2r")
+        top_x = keep.tile([P, 1], F32, name="top_x")
+        nc.vector.tensor_sub(out=rng[:], in0=big_bf[:], in1=m_bf[:])
+        nc.vector.reciprocal(out=rinv[:], in_=rng[:])
+        nc.vector.tensor_copy(out=big_f[:], in_=big_bf[:])
+        nc.vector.tensor_scalar_mul(out=c63[:], in0=rinv[:], scalar1=63.0)
+        nc.vector.tensor_scalar_mul(out=neg_2r[:], in0=rng[:], scalar1=-2.0)
+        nc.vector.tensor_mul(out=mc[:], in0=m_bf[:], in1=c63[:])
+        nc.vector.tensor_scalar_mul(out=neg_r[:], in0=rng[:], scalar1=-1.0)
+        nc.vector.tensor_scalar(out=tabr[:], in0=tab0[:, 0:9], scalar1=mc[:, 0:1], scalar2=None, op0=ALU.subtract)
+        nc.vector.scalar_tensor_tensor(
+            out=top_x[:], in0=rng[:], scalar=3.5, in1=big_f[:], op0=ALU.mult, op1=ALU.add
+        )
+
+        xf = keep.tile([P, 2, F, 4], F32, name="xf")
+        above = keep.tile([P, 2, F, 4], F32, name="above")
+        side = keep.tile([P, 2, F, 4], F32, name="side")
+        xe = keep.tile([P, 2, F, 4], F32, name="xe")
+        fold1 = keep.tile([P, 2, F, 4], F32, name="fold1")
+        fold2 = keep.tile([P, 2, F, 4], F32, name="fold2")
+        fold3 = keep.tile([P, 2, F, 2, 4], F32, name="fold3")
+
+        def token_level(f0, f1):
+            nc.vector.tensor_copy(out=xf[:, :, f0:f1, :], in_=x_sb[:, :, :, f0:f1].rearrange("p g t f -> p g f t"))
+            nc.vector.tensor_scalar(
+                out=above[:, :, f0:f1, :], in0=xf[:, :, f0:f1, :], scalar1=big_f[:, 0:1], scalar2=None, op0=ALU.is_gt
+            )
+            nc.vector.scalar_tensor_tensor(
+                out=side[:, :, f0:f1, :],
+                in0=xf[:, :, f0:f1, :],
+                scalar=m_bf[:, 0:1],
+                in1=above[:, :, f0:f1, :],
+                op0=ALU.is_lt,
+                op1=ALU.subtract,
+            )
+            nc.vector.scalar_tensor_tensor(
+                out=xe[:, :, f0:f1, :],
+                in0=side[:, :, f0:f1, :],
+                scalar=neg_2r[:, 0:1],
+                in1=xf[:, :, f0:f1, :],
+                op0=ALU.mult,
+                op1=ALU.add,
+            )
+
+        def folds(f0, f1):
+            nc.scalar.activation(
+                out=fold1[:, :, f0:f1, :], in_=xf[:, :, f0:f1, :], func=ACT.Abs, bias=tabr[:, 8:9], scale=c63[:, 0:1]
+            )
+            nc.scalar.activation(
+                out=fold2[:, :, f0:f1, :], in_=fold1[:, :, f0:f1, :], func=ACT.Abs, bias=tab0[:, 9:10], scale=1.0
+            )
+            nc.scalar.activation(
+                out=fold3[:, :, f0:f1, 1, :], in_=fold2[:, :, f0:f1, :], func=ACT.Abs, bias=tab0[:, 10:11], scale=1.0
+            )
+            nc.scalar.activation(
+                out=fold3[:, :, f0:f1, 0, :],
+                in_=fold3[:, :, f0:f1, 1, :],
+                func=ACT.Identity,
+                bias=tab0[:, 11:12],
+                scale=-1.0,
+            )
+
+        leaves = {}
+
+        def planes(gi):
+            grp = GROUPS[gi]
+            nf = 8 * len(grp)
+            f0 = 8 * grp[0]
+            abs_x = keep.tile([P, 2, nf, 8, 4], F32, name="abs_x%d" % gi)
+            abs_y = keep.tile([P, 2, nf, 2, 8, 4], F32, name="abs_y%d" % gi)
+            for a in range(8):
+                nc.scalar.activation(
+                    out=abs_x[:, :, :, a, :],
+                    in_=xe[:, :, f0 : f0 + nf, :],
+                    func=ACT.Abs,
+                    bias=tabr[:, a : a + 1],
+                    scale=c63[:, 0:1],
+                )
+            for c in range(8):
+                nc.scalar.activation(
+                    out=abs_y[:, :, :, :, c, :],
+                    in_=fold3[:, :, f0 : f0 + nf, :, :],
+                    func=ACT.Abs,
+                    bias=tab0[:, 12 + c : 13 + c],
+                    scale=1.0,
+                )
+            leaves[gi] = (abs_x, abs_y)
+
+        def finish_leaves(gi):
+            grp = GROUPS[gi]
+            nf = 8 * len(grp)
+            abs_x, abs_y = leaves[gi]
+            row = keep.tile([P, 2, nf, 8, 4], BF16, name="row%d" % gi)
+            col = keep.tile([P, 2, nf, 2, 8, 4], BF16, name="col%d" % gi)
+            nc.vector.tensor_scalar(
+                out=row[:], in0=abs_x[:], scalar1=neg_r[:, 0:1], scalar2=top_x[:, 0:1], op0=ALU.mult, op1=ALU.add
+            )
+            nc.vector.tensor_scalar(
+                out=col[:], in0=abs_y[:], scalar1=neg_r[:, 0:1], scalar2=big_f[:, 0:1], op0=ALU.mult, op1=ALU.add
+            )
+            nc.vector.tensor_scalar(
+                out=row[:], in0=row[:], scalar1=big_bf[:, 0:1], scalar2=m_bf[:, 0:1], op0=ALU.min, op1=ALU.max
+            )
+            nc.vector.tensor_scalar(out=col[:], in0=col[:], scalar1=m_bf[:, 0:1], scalar2=None, op0=ALU.max)
+            leaves[gi] = (row, col)
+
+        g_grp = keep.tile([P, 2, N_CLS, 4], BF16, name="g_grp", align_bytes=64)
+        g_codes = keep.tile([P, 2, N_CLS], U32, name="g_codes", align_bytes=64)
+        g_scales = keep.tile([P, 2, N_CLS], U8, name="g_scales", align_bytes=64)
+
+        def regroup(eng, g, h):
+            n0 = 512 * h
+            dst = g_grp[:, g, n0 : n0 + 512, :].rearrange("p (c i) t -> p c t i", i=4)
+            src = g_raw[:, g, :, n0 : n0 + 512].rearrange("p t (c i) -> p c t i", i=4)
+            if eng == "v":
+                nc.vector.tensor_copy(out=dst, in_=src)
+            else:
+                nc.scalar.copy(out=dst, in_=src)
+
+        def quantise_g(g, h):
+            n0 = 512 * h
+            nc.vector.quantize_mx(
+                out=g_codes[:, g, n0 : n0 + 512].bitcast(E5X4),
+                scales=g_scales[:, g, n0 : n0 + 512],
+                in_=g_grp[:, g, n0 : n0 + 512, :].rearrange("p n j -> p (n j)"),
+            )
+
+        emb_codes = {}
+
+        def produce(fo):
+            gi = [i for i, grp in enumerate(GROUPS) if fo in grp][0]
+            q0 = 8 * (fo - GROUPS[gi][0])
+            row, col = leaves[gi]
+            emb = embp.tile([P, 2, 2048], BF16, name="emb", align_bytes=64)
+            codes = codep.tile([P, 2, 512], U32, name="codes", align_bytes=64)
+            scales = codep.tile([P, 2, 512], U8, name="scales", align_bytes=64)
+            shape = [P, 8, 4, 2, 8, 4]
+            for g in range(2):
+                nc.vector.tensor_tensor(
+                    out=emb[:, g, :].rearrange("p (q h r c t) -> p q h r c t", q=8, h=4, r=2, c=8, t=4),
+                    in0=row[:, g, q0 : q0 + 8, :, :]
+                    .rearrange("p q (h r) t -> p q h r t", h=4, r=2)
+                    .unsqueeze(4)
+                    .to_broadcast(shape),
+                    in1=col[:, g, q0 : q0 + 8, :, :, :].unsqueeze(2).to_broadcast(shape),
+                    op=ALU.min,
+                )
+            for g in range(2):
+                nc.vector.quantize_mx(out=codes[:, g, :].bitcast(E4X4), scales=scales[:, g, :], in_=emb[:, g, :])
+            emb_codes[fo] = (codes, scales)
+
+        def one_pass(acc, fo, nt, g):
+            codes, scales = emb_codes[fo]
+            nc.tensor.matmul_mx(
+                out=acc[:],
+                lhsT=g_codes[:, g, nt * P : (nt + 1) * P].bitcast(E5X4),
+                lhsT_scale=g_scales[:, g, nt * P : (nt + 1) * P],
+                rhs=codes[:, g, :].bitcast(E4X4),
+                rhs_scale=scales[:, g, :],
+                start=(g == 0),
+                stop=(g == 1),
+            )
+
+        def drain(acc, fo, nt):
+            stage = stagep.tile([P, 512], F32, name="stage")
+            if nt in VECTOR_BANKS[fo]:
+                nc.vector.tensor_copy(out=stage[:], in_=acc[:])
+            else:
+                nc.scalar.copy(out=stage[:], in_=acc[:])
+            nc.sync.dma_start(out=out[nt * P : (nt + 1) * P, fo * 512 : (fo + 1) * 512], in_=stage[:])
+
+        def round_of(fo):
+            for nt in range(8):
+                acc = psum.tile([P, 512], F32, name="acc")
+                one_pass(acc, fo, nt, 0)
+                one_pass(acc, fo, nt, 1)
+                drain(acc, fo, nt)
+
+        token_level(0, 8)
+        folds(0, 8)
+        planes(0)
+        token_level(8, F)
+        folds(8, F)
+        regroup("v", 0, 0)
+        regroup("v", 0, 1)
+        regroup("s", 1, 0)
+        regroup("s", 1, 1)
+        finish_leaves(0)
+        produce(0)
+        for g in range(2):
+            for h in range(2):
+                quantise_g(g, h)
+        for gi in range(1, len(GROUPS)):
+            planes(gi)
+        for fo in range(8):
+            round_of(fo)
+            if fo + 1 < 8:
+                starts = [i for i, grp in enumerate(GROUPS) if grp[0] == fo + 1]
+                if starts:
+                    finish_leaves(starts[0])
+                produce(fo + 1)

@@ -18,7 +18,7 @@ FLOPS = 2 * B * N_CLS * K
 BYTES = 4 * N_CLS * K + 2 * B * N_CLS + 2 * B * F + 4
 
 GROUPS = ((0,), (1,), (2, 3), (4, 5, 6, 7))
-VECTOR_BANKS = {0: (7,), 1: (7,), 2: (7,), 3: (7,), 4: (7,), 5: (7,), 6: (7,), 7: (1, 3, 5, 7)}
+VECTOR_BANKS = {7: (1, 3, 5, 7)}
 
 
 def tile_lagrangenet_kernel(tc, x, min_x, max_x, W, dof, grad_out, out):
@@ -26,10 +26,11 @@ def tile_lagrangenet_kernel(tc, x, min_x, max_x, W, dof, grad_out, out):
     assert dof == DOF
     with ExitStack() as ctx:
         keep = ctx.enter_context(tc.tile_pool(name="keep", bufs=1))
-        embp = ctx.enter_context(tc.tile_pool(name="embp", bufs=3))
+        embp = ctx.enter_context(tc.tile_pool(name="embp", bufs=2))
         codep = ctx.enter_context(tc.tile_pool(name="codep", bufs=4))
-        stagep = ctx.enter_context(tc.tile_pool(name="stagep", bufs=12))
+        stagep = ctx.enter_context(tc.tile_pool(name="stagep", bufs=10))
         psum = ctx.enter_context(tc.psum_pool(name="acc", bufs=8))
+        ctx.enter_context(tc.manual_schedule())
 
         m_bf = keep.tile([P, 1], BF16, name="m_bf")
         big_bf = keep.tile([P, 1], BF16, name="big_bf")
@@ -44,8 +45,8 @@ def tile_lagrangenet_kernel(tc, x, min_x, max_x, W, dof, grad_out, out):
                 in_=grad_out[g * 512 : (g + 1) * 512, :].rearrange("(p j) n -> p j n", j=4),
             )
 
-        tab0 = keep.tile([P, 20], F32, name="tab0")
-        consts = [-(8.0 * a + 3.5) for a in range(8)] + [-31.5, -16.0, -8.0, 8.0] + [-(c + 0.5) for c in range(8)]
+        tab0 = keep.tile([P, 19], F32, name="tab0")
+        consts = [-(8.0 * a + 3.5) for a in range(8)] + [-31.5, -16.0, -8.0] + [-(c + 0.5) for c in range(8)]
         for j, v in enumerate(consts):
             nc.vector.memset(tab0[:, j : j + 1], v)
         warm = keep.tile([P, 1], F32, name="warm")
@@ -78,7 +79,7 @@ def tile_lagrangenet_kernel(tc, x, min_x, max_x, W, dof, grad_out, out):
         xe = keep.tile([P, 2, F, 4], F32, name="xe")
         fold1 = keep.tile([P, 2, F, 4], F32, name="fold1")
         fold2 = keep.tile([P, 2, F, 4], F32, name="fold2")
-        fold3 = keep.tile([P, 2, F, 2, 4], F32, name="fold3")
+        fold3 = keep.tile([P, 2, F, 4], F32, name="fold3")
 
         def token_level(f0, f1):
             nc.vector.tensor_copy(out=xf[:, :, f0:f1, :], in_=x_sb[:, :, :, f0:f1].rearrange("p g t f -> p g f t"))
@@ -110,99 +111,104 @@ def tile_lagrangenet_kernel(tc, x, min_x, max_x, W, dof, grad_out, out):
                 out=fold2[:, :, f0:f1, :], in_=fold1[:, :, f0:f1, :], func=ACT.Abs, bias=tab0[:, 9:10], scale=1.0
             )
             nc.scalar.activation(
-                out=fold3[:, :, f0:f1, 1, :], in_=fold2[:, :, f0:f1, :], func=ACT.Abs, bias=tab0[:, 10:11], scale=1.0
-            )
-            nc.scalar.activation(
-                out=fold3[:, :, f0:f1, 0, :],
-                in_=fold3[:, :, f0:f1, 1, :],
-                func=ACT.Identity,
-                bias=tab0[:, 11:12],
-                scale=-1.0,
+                out=fold3[:, :, f0:f1, :], in_=fold2[:, :, f0:f1, :], func=ACT.Abs, bias=tab0[:, 10:11], scale=1.0
             )
 
         leaves = {}
 
-        def planes(gi):
+        def plane_jobs(gi):
             grp = GROUPS[gi]
-            nf = 8 * len(grp)
+            nfo = len(grp)
             f0 = 8 * grp[0]
-            abs_x = keep.tile([P, 2, nf, 8, 4], F32, name="abs_x%d" % gi)
-            abs_y = keep.tile([P, 2, nf, 2, 8, 4], F32, name="abs_y%d" % gi)
-            for a in range(8):
+            f1 = f0 + 8 * nfo
+            abs_x = keep.tile([P, 2, nfo, 8, 32], F32, name="abs_x%d" % gi)
+            abs_y = keep.tile([P, 2, nfo, 8, 32], F32, name="abs_y%d" % gi)
+            leaves[gi] = (abs_x, abs_y)
+
+            def x_plane(a):
                 nc.scalar.activation(
                     out=abs_x[:, :, :, a, :],
-                    in_=xe[:, :, f0 : f0 + nf, :],
+                    in_=xe[:, :, f0:f1, :].rearrange("p g (o l) t -> p g o (l t)", o=nfo),
                     func=ACT.Abs,
                     bias=tabr[:, a : a + 1],
                     scale=c63[:, 0:1],
                 )
-            for c in range(8):
+
+            def y_plane(c):
                 nc.scalar.activation(
-                    out=abs_y[:, :, :, :, c, :],
-                    in_=fold3[:, :, f0 : f0 + nf, :, :],
+                    out=abs_y[:, :, :, c, :],
+                    in_=fold3[:, :, f0:f1, :].rearrange("p g (o l) t -> p g o (l t)", o=nfo),
                     func=ACT.Abs,
-                    bias=tab0[:, 12 + c : 13 + c],
+                    bias=tab0[:, 11 + c : 12 + c],
                     scale=1.0,
                 )
-            leaves[gi] = (abs_x, abs_y)
+
+            return [(x_plane, a) for a in range(8)] + [(y_plane, c) for c in range(8)]
+
+        def planes(gi):
+            for job, k in plane_jobs(gi):
+                job(k)
 
         def finish_leaves(gi):
-            grp = GROUPS[gi]
-            nf = 8 * len(grp)
+            nfo = len(GROUPS[gi])
             abs_x, abs_y = leaves[gi]
-            row = keep.tile([P, 2, nf, 8, 4], BF16, name="row%d" % gi)
-            col = keep.tile([P, 2, nf, 2, 8, 4], BF16, name="col%d" % gi)
+            row = keep.tile([P, 2, nfo, 8, 32], BF16, name="row%d" % gi)
+            colr = keep.tile([P, 2, nfo, 8, 32], BF16, name="colr%d" % gi)
+            col2 = keep.tile([P, 2, nfo, 2, 8, 32], BF16, name="col2%d" % gi)
             nc.vector.tensor_scalar(
                 out=row[:], in0=abs_x[:], scalar1=neg_r[:, 0:1], scalar2=top_x[:, 0:1], op0=ALU.mult, op1=ALU.add
             )
             nc.vector.tensor_scalar(
-                out=col[:], in0=abs_y[:], scalar1=neg_r[:, 0:1], scalar2=big_f[:, 0:1], op0=ALU.mult, op1=ALU.add
+                out=colr[:], in0=abs_y[:], scalar1=neg_r[:, 0:1], scalar2=big_f[:, 0:1], op0=ALU.mult, op1=ALU.add
             )
+            nc.vector.tensor_scalar(out=row[:], in0=row[:], scalar1=m_bf[:, 0:1], scalar2=None, op0=ALU.max)
             nc.vector.tensor_scalar(
-                out=row[:], in0=row[:], scalar1=big_bf[:, 0:1], scalar2=m_bf[:, 0:1], op0=ALU.min, op1=ALU.max
+                out=col2[:, :, :, 1, :, :], in0=colr[:], scalar1=m_bf[:, 0:1], scalar2=None, op0=ALU.max
             )
-            nc.vector.tensor_scalar(out=col[:], in0=col[:], scalar1=m_bf[:, 0:1], scalar2=None, op0=ALU.max)
-            leaves[gi] = (row, col)
+            for c in range(8):
+                nc.vector.tensor_scalar(
+                    out=col2[:, :, :, 0, 7 - c, :],
+                    in0=colr[:, :, :, c, :],
+                    scalar1=m_bf[:, 0:1],
+                    scalar2=None,
+                    op0=ALU.max,
+                )
+            leaves[gi] = (row, col2)
 
         g_grp = keep.tile([P, 2, N_CLS, 4], BF16, name="g_grp", align_bytes=64)
         g_codes = keep.tile([P, 2, N_CLS], U32, name="g_codes", align_bytes=64)
         g_scales = keep.tile([P, 2, N_CLS], U8, name="g_scales", align_bytes=64)
 
-        def regroup(eng, g, h):
-            n0 = 512 * h
-            dst = g_grp[:, g, n0 : n0 + 512, :].rearrange("p (c i) t -> p c t i", i=4)
-            src = g_raw[:, g, :, n0 : n0 + 512].rearrange("p t (c i) -> p c t i", i=4)
-            if eng == "v":
-                nc.vector.tensor_copy(out=dst, in_=src)
-            else:
-                nc.scalar.copy(out=dst, in_=src)
+        def regroup(g, qd):
+            n0 = 256 * qd
+            nc.vector.tensor_copy(
+                out=g_grp[:, g, n0 : n0 + 256, :].rearrange("p (c i) t -> p c t i", i=4),
+                in_=g_raw[:, g, :, n0 : n0 + 256].rearrange("p t (c i) -> p c t i", i=4),
+            )
 
-        def quantise_g(g, h):
-            n0 = 512 * h
+        def quantise_g(g, qd):
+            n0 = 256 * qd
             nc.vector.quantize_mx(
-                out=g_codes[:, g, n0 : n0 + 512].bitcast(E5X4),
-                scales=g_scales[:, g, n0 : n0 + 512],
-                in_=g_grp[:, g, n0 : n0 + 512, :].rearrange("p n j -> p (n j)"),
+                out=g_codes[:, g, n0 : n0 + 256].bitcast(E5X4),
+                scales=g_scales[:, g, n0 : n0 + 256],
+                in_=g_grp[:, g, n0 : n0 + 256, :].rearrange("p n j -> p (n j)"),
             )
 
         emb_codes = {}
 
         def produce(fo):
             gi = [i for i, grp in enumerate(GROUPS) if fo in grp][0]
-            q0 = 8 * (fo - GROUPS[gi][0])
-            row, col = leaves[gi]
+            j = fo - GROUPS[gi][0]
+            row, col2 = leaves[gi]
             emb = embp.tile([P, 2, 2048], BF16, name="emb", align_bytes=64)
             codes = codep.tile([P, 2, 512], U32, name="codes", align_bytes=64)
             scales = codep.tile([P, 2, 512], U8, name="scales", align_bytes=64)
-            shape = [P, 8, 4, 2, 8, 4]
+            shape = [P, 4, 2, 8, 32]
             for g in range(2):
                 nc.vector.tensor_tensor(
-                    out=emb[:, g, :].rearrange("p (q h r c t) -> p q h r c t", q=8, h=4, r=2, c=8, t=4),
-                    in0=row[:, g, q0 : q0 + 8, :, :]
-                    .rearrange("p q (h r) t -> p q h r t", h=4, r=2)
-                    .unsqueeze(4)
-                    .to_broadcast(shape),
-                    in1=col[:, g, q0 : q0 + 8, :, :, :].unsqueeze(2).to_broadcast(shape),
+                    out=emb[:, g, :].rearrange("p (h r c x) -> p h r c x", h=4, r=2, c=8, x=32),
+                    in0=row[:, g, j].rearrange("p (h r) x -> p h r x", h=4, r=2).unsqueeze(3).to_broadcast(shape),
+                    in1=col2[:, g, j].unsqueeze(1).to_broadcast(shape),
                     op=ALU.min,
                 )
             for g in range(2):
@@ -221,41 +227,59 @@ def tile_lagrangenet_kernel(tc, x, min_x, max_x, W, dof, grad_out, out):
                 stop=(g == 1),
             )
 
+        late_jobs = []
+        cursor = [0]
+
         def drain(acc, fo, nt):
             stage = stagep.tile([P, 512], F32, name="stage")
-            if nt in VECTOR_BANKS[fo]:
-                nc.vector.tensor_copy(out=stage[:], in_=acc[:])
+            src = acc[:].rearrange("p (k l) -> p l k", l=8)
+            dst = stage[:].rearrange("p (l k) -> p l k", l=8)
+            if nt in VECTOR_BANKS.get(fo, ()):
+                nc.vector.tensor_copy(out=dst, in_=src)
             else:
-                nc.scalar.copy(out=stage[:], in_=acc[:])
+                nc.scalar.copy(out=dst, in_=src)
+                if cursor[0] < len(late_jobs):
+                    job, k = late_jobs[cursor[0]]
+                    cursor[0] += 1
+                    job(k)
             nc.sync.dma_start(out=out[nt * P : (nt + 1) * P, fo * 512 : (fo + 1) * 512], in_=stage[:])
 
-        def round_of(fo):
-            for nt in range(8):
-                acc = psum.tile([P, 512], F32, name="acc")
-                one_pass(acc, fo, nt, 0)
-                one_pass(acc, fo, nt, 1)
-                drain(acc, fo, nt)
+        def group_of(fo, nt):
+            acc = psum.tile([P, 512], F32, name="acc")
+            one_pass(acc, fo, nt, 0)
+            one_pass(acc, fo, nt, 1)
+            drain(acc, fo, nt)
 
         token_level(0, 8)
         folds(0, 8)
         planes(0)
         token_level(8, F)
         folds(8, F)
-        regroup("v", 0, 0)
-        regroup("v", 0, 1)
-        regroup("s", 1, 0)
-        regroup("s", 1, 1)
+        planes(1)
+        planes(2)
+        late_jobs.extend(plane_jobs(3))
         finish_leaves(0)
         produce(0)
-        for g in range(2):
-            for h in range(2):
-                quantise_g(g, h)
-        for gi in range(1, len(GROUPS)):
-            planes(gi)
-        for fo in range(8):
-            round_of(fo)
-            if fo + 1 < 8:
-                starts = [i for i, grp in enumerate(GROUPS) if grp[0] == fo + 1]
-                if starts:
-                    finish_leaves(starts[0])
-                produce(fo + 1)
+        for qd in range(4):
+            regroup(0, qd)
+            regroup(1, qd)
+            quantise_g(0, qd)
+            quantise_g(1, qd)
+            group_of(0, 2 * qd)
+            group_of(0, 2 * qd + 1)
+        for fo in range(1, 7):
+            starts = [i for i, grp in enumerate(GROUPS) if grp[0] == fo]
+            if starts:
+                finish_leaves(starts[0])
+            produce(fo)
+            for nt in range(8):
+                group_of(fo, nt)
+        produce(7)
+        accs = []
+        for nt in range(8):
+            acc = psum.tile([P, 512], F32, name="acc")
+            accs.append(acc)
+            one_pass(acc, 7, nt, 0)
+        for nt in range(8):
+            one_pass(accs[nt], 7, nt, 1)
+            drain(accs[nt], 7, nt)

@@ -18,7 +18,8 @@ FLOPS = 2 * B * N_CLS * K
 BYTES = 4 * N_CLS * K + 2 * B * N_CLS + 2 * B * F + 4
 
 GROUPS = ((0,), (1,), (2, 3), (4, 5, 6, 7))
-VECTOR_BANKS = {7: (1, 3, 5, 7)}
+VECTOR_BANKS = {1: (3,), 2: (3,), 3: (3,), 4: (3,), 5: (3,), 6: (3,), 7: (1, 3, 5, 7)}
+PINNED = False
 
 
 def tile_lagrangenet_kernel(tc, x, min_x, max_x, W, dof, grad_out, out):
@@ -30,7 +31,8 @@ def tile_lagrangenet_kernel(tc, x, min_x, max_x, W, dof, grad_out, out):
         codep = ctx.enter_context(tc.tile_pool(name="codep", bufs=4))
         stagep = ctx.enter_context(tc.tile_pool(name="stagep", bufs=10))
         psum = ctx.enter_context(tc.psum_pool(name="acc", bufs=8))
-        ctx.enter_context(tc.manual_schedule())
+        if PINNED:
+            ctx.enter_context(tc.manual_schedule())
 
         m_bf = keep.tile([P, 1], BF16, name="m_bf")
         big_bf = keep.tile([P, 1], BF16, name="big_bf")
@@ -53,22 +55,30 @@ def tile_lagrangenet_kernel(tc, x, min_x, max_x, W, dof, grad_out, out):
         nc.scalar.activation(out=warm[:], in_=tab0[:, 0:1], func=ACT.Abs)
 
         big_f = keep.tile([P, 1], F32, name="big_f")
+        neg_m = keep.tile([P, 1], F32, name="neg_m")
+        n63m = keep.tile([P, 1], F32, name="n63m")
         rng = keep.tile([P, 1], F32, name="rng")
+        tab_a = keep.tile([P, 8], F32, name="tab_a")
+        tab_y = keep.tile([P, 8], F32, name="tab_y")
         rinv = keep.tile([P, 1], F32, name="rinv")
         c63 = keep.tile([P, 1], F32, name="c63")
         mc = keep.tile([P, 1], F32, name="mc")
-        tabr = keep.tile([P, 9], F32, name="tabr")
-        neg_r = keep.tile([P, 1], F32, name="neg_r")
+        bias1 = keep.tile([P, 1], F32, name="bias1")
         neg_2r = keep.tile([P, 1], F32, name="neg_2r")
         top_x = keep.tile([P, 1], F32, name="top_x")
         nc.vector.tensor_sub(out=rng[:], in0=big_bf[:], in1=m_bf[:])
         nc.vector.reciprocal(out=rinv[:], in_=rng[:])
-        nc.vector.tensor_copy(out=big_f[:], in_=big_bf[:])
+        nc.vector.tensor_scalar_mul(out=n63m[:], in0=m_bf[:], scalar1=-63.0)
         nc.vector.tensor_scalar_mul(out=c63[:], in0=rinv[:], scalar1=63.0)
         nc.vector.tensor_scalar_mul(out=neg_2r[:], in0=rng[:], scalar1=-2.0)
         nc.vector.tensor_mul(out=mc[:], in0=m_bf[:], in1=c63[:])
-        nc.vector.tensor_scalar_mul(out=neg_r[:], in0=rng[:], scalar1=-1.0)
-        nc.vector.tensor_scalar(out=tabr[:], in0=tab0[:, 0:9], scalar1=mc[:, 0:1], scalar2=None, op0=ALU.subtract)
+        nc.vector.tensor_scalar(
+            out=tab_a[:], in0=tab0[:, 0:8], scalar1=rng[:, 0:1], scalar2=n63m[:, 0:1], op0=ALU.mult, op1=ALU.add
+        )
+        nc.vector.tensor_sub(out=bias1[:], in0=tab0[:, 8:9], in1=mc[:])
+        nc.vector.tensor_copy(out=big_f[:], in_=big_bf[:])
+        nc.vector.tensor_scalar(out=tab_y[:], in0=tab0[:, 11:19], scalar1=rng[:, 0:1], scalar2=None, op0=ALU.mult)
+        nc.vector.tensor_scalar_mul(out=neg_m[:], in0=m_bf[:], scalar1=-1.0)
         nc.vector.scalar_tensor_tensor(
             out=top_x[:], in0=rng[:], scalar=3.5, in1=big_f[:], op0=ALU.mult, op1=ALU.add
         )
@@ -105,7 +115,7 @@ def tile_lagrangenet_kernel(tc, x, min_x, max_x, W, dof, grad_out, out):
 
         def folds(f0, f1):
             nc.scalar.activation(
-                out=fold1[:, :, f0:f1, :], in_=xf[:, :, f0:f1, :], func=ACT.Abs, bias=tabr[:, 8:9], scale=c63[:, 0:1]
+                out=fold1[:, :, f0:f1, :], in_=xf[:, :, f0:f1, :], func=ACT.Abs, bias=bias1[:, 0:1], scale=c63[:, 0:1]
             )
             nc.scalar.activation(
                 out=fold2[:, :, f0:f1, :], in_=fold1[:, :, f0:f1, :], func=ACT.Abs, bias=tab0[:, 9:10], scale=1.0
@@ -130,8 +140,8 @@ def tile_lagrangenet_kernel(tc, x, min_x, max_x, W, dof, grad_out, out):
                     out=abs_x[:, :, :, a, :],
                     in_=xe[:, :, f0:f1, :].rearrange("p g (o l) t -> p g o (l t)", o=nfo),
                     func=ACT.Abs,
-                    bias=tabr[:, a : a + 1],
-                    scale=c63[:, 0:1],
+                    bias=tab_a[:, a : a + 1],
+                    scale=63.0,
                 )
 
             def y_plane(c):
@@ -139,8 +149,8 @@ def tile_lagrangenet_kernel(tc, x, min_x, max_x, W, dof, grad_out, out):
                     out=abs_y[:, :, :, c, :],
                     in_=fold3[:, :, f0:f1, :].rearrange("p g (o l) t -> p g o (l t)", o=nfo),
                     func=ACT.Abs,
-                    bias=tab0[:, 11 + c : 12 + c],
-                    scale=1.0,
+                    bias=tab_y[:, c : c + 1],
+                    scale=rng[:, 0:1],
                 )
 
             return [(x_plane, a) for a in range(8)] + [(y_plane, c) for c in range(8)]
@@ -153,26 +163,23 @@ def tile_lagrangenet_kernel(tc, x, min_x, max_x, W, dof, grad_out, out):
             nfo = len(GROUPS[gi])
             abs_x, abs_y = leaves[gi]
             row = keep.tile([P, 2, nfo, 8, 32], BF16, name="row%d" % gi)
-            colr = keep.tile([P, 2, nfo, 8, 32], BF16, name="colr%d" % gi)
             col2 = keep.tile([P, 2, nfo, 2, 8, 32], BF16, name="col2%d" % gi)
             nc.vector.tensor_scalar(
-                out=row[:], in0=abs_x[:], scalar1=neg_r[:, 0:1], scalar2=top_x[:, 0:1], op0=ALU.mult, op1=ALU.add
+                out=col2[:, :, :, 1, :, :],
+                in0=abs_y[:],
+                scalar1=big_f[:, 0:1],
+                scalar2=neg_m[:, 0:1],
+                op0=ALU.subtract,
+                op1=ALU.min,
             )
             nc.vector.tensor_scalar(
-                out=colr[:], in0=abs_y[:], scalar1=neg_r[:, 0:1], scalar2=big_f[:, 0:1], op0=ALU.mult, op1=ALU.add
-            )
-            nc.vector.tensor_scalar(out=row[:], in0=row[:], scalar1=m_bf[:, 0:1], scalar2=None, op0=ALU.max)
-            nc.vector.tensor_scalar(
-                out=col2[:, :, :, 1, :, :], in0=colr[:], scalar1=m_bf[:, 0:1], scalar2=None, op0=ALU.max
+                out=row[:], in0=abs_x[:], scalar1=top_x[:, 0:1], scalar2=neg_m[:, 0:1], op0=ALU.subtract, op1=ALU.min
             )
             for c in range(8):
-                nc.vector.tensor_scalar(
-                    out=col2[:, :, :, 0, 7 - c, :],
-                    in0=colr[:, :, :, c, :],
-                    scalar1=m_bf[:, 0:1],
-                    scalar2=None,
-                    op0=ALU.max,
-                )
+                if gi == 0:
+                    nc.vector.tensor_copy(out=col2[:, :, :, 0, 7 - c, :], in_=col2[:, :, :, 1, c, :])
+                else:
+                    nc.scalar.copy(out=col2[:, :, :, 0, 7 - c, :], in_=col2[:, :, :, 1, c, :])
             leaves[gi] = (row, col2)
 
         g_grp = keep.tile([P, 2, N_CLS, 4], BF16, name="g_grp", align_bytes=64)
@@ -181,10 +188,12 @@ def tile_lagrangenet_kernel(tc, x, min_x, max_x, W, dof, grad_out, out):
 
         def regroup(g, qd):
             n0 = 256 * qd
-            nc.vector.tensor_copy(
-                out=g_grp[:, g, n0 : n0 + 256, :].rearrange("p (c i) t -> p c t i", i=4),
-                in_=g_raw[:, g, :, n0 : n0 + 256].rearrange("p t (c i) -> p c t i", i=4),
-            )
+            dst = g_grp[:, g, n0 : n0 + 256, :].rearrange("p (c i) t -> p c t i", i=4)
+            src = g_raw[:, g, :, n0 : n0 + 256].rearrange("p t (c i) -> p c t i", i=4)
+            if g == 0 or qd >= 2:
+                nc.vector.tensor_scalar(out=dst, in0=src, scalar1=-1.0, scalar2=None, op0=ALU.mult)
+            else:
+                nc.scalar.mul(out=dst, in_=src, mul=-1.0)
 
         def quantise_g(g, qd):
             n0 = 256 * qd
@@ -209,7 +218,7 @@ def tile_lagrangenet_kernel(tc, x, min_x, max_x, W, dof, grad_out, out):
                     out=emb[:, g, :].rearrange("p (h r c x) -> p h r c x", h=4, r=2, c=8, x=32),
                     in0=row[:, g, j].rearrange("p (h r) x -> p h r x", h=4, r=2).unsqueeze(3).to_broadcast(shape),
                     in1=col2[:, g, j].unsqueeze(1).to_broadcast(shape),
-                    op=ALU.min,
+                    op=ALU.max,
                 )
             for g in range(2):
                 nc.vector.quantize_mx(out=codes[:, g, :].bitcast(E4X4), scales=scales[:, g, :], in_=emb[:, g, :])
@@ -250,31 +259,42 @@ def tile_lagrangenet_kernel(tc, x, min_x, max_x, W, dof, grad_out, out):
             one_pass(acc, fo, nt, 1)
             drain(acc, fo, nt)
 
-        token_level(0, 8)
-        folds(0, 8)
+        def bounds(gi):
+            return 8 * GROUPS[gi][0], 8 * GROUPS[gi][-1] + 8
+
+        token_level(*bounds(0))
+        folds(*bounds(0))
         planes(0)
-        token_level(8, F)
-        folds(8, F)
+        token_level(*bounds(1))
+        folds(*bounds(1))
         planes(1)
+        finish_leaves(0)
+        for qd in range(2):
+            regroup(1, qd)
+        produce(0)
+        for gi in range(2, len(GROUPS)):
+            token_level(*bounds(gi))
+            folds(*bounds(gi))
         planes(2)
         late_jobs.extend(plane_jobs(3))
-        finish_leaves(0)
-        produce(0)
         for qd in range(4):
             regroup(0, qd)
-            regroup(1, qd)
+            if qd >= 2:
+                regroup(1, qd)
             quantise_g(0, qd)
             quantise_g(1, qd)
+            if qd == 0:
+                finish_leaves(1)
             group_of(0, 2 * qd)
             group_of(0, 2 * qd + 1)
+        produce(1)
         for fo in range(1, 7):
-            starts = [i for i, grp in enumerate(GROUPS) if grp[0] == fo]
+            starts = [i for i, grp in enumerate(GROUPS) if grp[0] == fo + 1]
             if starts:
                 finish_leaves(starts[0])
-            produce(fo)
+            produce(fo + 1)
             for nt in range(8):
                 group_of(fo, nt)
-        produce(7)
         accs = []
         for nt in range(8):
             acc = psum.tile([P, 512], F32, name="acc")

@@ -190,7 +190,7 @@ def tile_lagrangenet_kernel(tc, x, min_x, max_x, W, dof, grad_out, out):
             n0 = 256 * qd
             dst = g_grp[:, g, n0 : n0 + 256, :].rearrange("p (c i) t -> p c t i", i=4)
             src = g_raw[:, g, :, n0 : n0 + 256].rearrange("p t (c i) -> p c t i", i=4)
-            if g == 0 or qd >= 2:
+            if g == 0:
                 nc.vector.tensor_scalar(out=dst, in0=src, scalar1=-1.0, scalar2=None, op0=ALU.mult)
             else:
                 nc.scalar.mul(out=dst, in_=src, mul=-1.0)
@@ -262,36 +262,34 @@ def tile_lagrangenet_kernel(tc, x, min_x, max_x, W, dof, grad_out, out):
         def bounds(gi):
             return 8 * GROUPS[gi][0], 8 * GROUPS[gi][-1] + 8
 
-        token_level(*bounds(0))
-        folds(*bounds(0))
-        planes(0)
-        token_level(*bounds(1))
-        folds(*bounds(1))
-        planes(1)
-        finish_leaves(0)
-        for qd in range(2):
-            regroup(1, qd)
-        produce(0)
-        for gi in range(2, len(GROUPS)):
+        def start_group(gi):
             token_level(*bounds(gi))
             folds(*bounds(gi))
-        planes(2)
-        late_jobs.extend(plane_jobs(3))
+            planes(gi)
+
+        start_group(0)
+        start_group(1)
+        finish_leaves(0)
+        for qd in range(4):
+            regroup(1, qd)
+        produce(0)
         for qd in range(4):
             regroup(0, qd)
-            if qd >= 2:
-                regroup(1, qd)
             quantise_g(0, qd)
             quantise_g(1, qd)
             if qd == 0:
                 finish_leaves(1)
             group_of(0, 2 * qd)
             group_of(0, 2 * qd + 1)
+        start_group(2)
         produce(1)
-        for fo in range(1, 7):
-            starts = [i for i, grp in enumerate(GROUPS) if grp[0] == fo + 1]
-            if starts:
-                finish_leaves(starts[0])
+        finish_leaves(2)
+        start_group(3)
+        produce(2)
+        for nt in range(8):
+            group_of(1, nt)
+        finish_leaves(3)
+        for fo in range(2, 7):
             produce(fo + 1)
             for nt in range(8):
                 group_of(fo, nt)

@@ -18,7 +18,7 @@ FLOPS = 2 * B * N_CLS * K
 BYTES = 4 * N_CLS * K + 2 * B * N_CLS + 2 * B * F + 4
 
 GROUPS = ((0,), (1,), (2, 3), (4, 5, 6, 7))
-VECTOR_BANKS = {1: (3,), 2: (3,), 3: (3,), 4: (3,), 5: (3,), 6: (3,), 7: (1, 3, 5, 7)}
+VECTOR_BANKS = {1: (3, 7), 2: (3, 7), 3: (3, 7), 4: (3, 7), 5: (3, 7), 6: (3, 7), 7: (1, 3, 5, 7)}
 PINNED = False
 
 
@@ -190,7 +190,7 @@ def tile_lagrangenet_kernel(tc, x, min_x, max_x, W, dof, grad_out, out):
             n0 = 256 * qd
             dst = g_grp[:, g, n0 : n0 + 256, :].rearrange("p (c i) t -> p c t i", i=4)
             src = g_raw[:, g, :, n0 : n0 + 256].rearrange("p t (c i) -> p c t i", i=4)
-            if g == 0:
+            if g >= 0:
                 nc.vector.tensor_scalar(out=dst, in0=src, scalar1=-1.0, scalar2=None, op0=ALU.mult)
             else:
                 nc.scalar.mul(out=dst, in_=src, mul=-1.0)
@@ -270,11 +270,10 @@ def tile_lagrangenet_kernel(tc, x, min_x, max_x, W, dof, grad_out, out):
         start_group(0)
         start_group(1)
         finish_leaves(0)
-        for qd in range(4):
-            regroup(1, qd)
         produce(0)
         for qd in range(4):
             regroup(0, qd)
+            regroup(1, qd)
             quantise_g(0, qd)
             quantise_g(1, qd)
             if qd == 0:

@@ -18,7 +18,7 @@ FLOPS = 2 * B * N_CLS * K
 BYTES = 4 * N_CLS * K + 2 * B * N_CLS + 2 * B * F + 4
 
 GROUPS = ((0,), (1,), (2, 3), (4, 5, 6, 7))
-VECTOR_BANKS = {1: (3, 7), 2: (3, 7), 3: (3, 7), 4: (3, 7), 5: (3, 7), 6: (3, 7), 7: (1, 3, 5, 7)}
+VECTOR_BANKS = {6: (1, 3, 5, 7), 7: (1, 3, 5, 7)}
 PINNED = False
 
 

@@ -17,7 +17,7 @@ K = F * DOF
 FLOPS = 2 * B * N_CLS * K
 BYTES = 4 * N_CLS * K + 2 * B * N_CLS + 2 * B * F + 4
 
-GROUPS = ((0,), (1,), (2, 3), (4, 5, 6, 7))
+GROUPS = ((0,), (1,), (2, 3), (4, 5), (6, 7))
 VECTOR_BANKS = {6: (1, 3, 5, 7), 7: (1, 3, 5, 7)}
 PINNED = False
 
@@ -176,7 +176,7 @@ def tile_lagrangenet_kernel(tc, x, min_x, max_x, W, dof, grad_out, out):
                 out=row[:], in0=abs_x[:], scalar1=top_x[:, 0:1], scalar2=neg_m[:, 0:1], op0=ALU.subtract, op1=ALU.min
             )
             for c in range(8):
-                if gi == 0:
+                if gi >= 0:
                     nc.vector.tensor_copy(out=col2[:, :, :, 0, 7 - c, :], in_=col2[:, :, :, 1, c, :])
                 else:
                     nc.scalar.copy(out=col2[:, :, :, 0, 7 - c, :], in_=col2[:, :, :, 1, c, :])
@@ -190,7 +190,7 @@ def tile_lagrangenet_kernel(tc, x, min_x, max_x, W, dof, grad_out, out):
             n0 = 256 * qd
             dst = g_grp[:, g, n0 : n0 + 256, :].rearrange("p (c i) t -> p c t i", i=4)
             src = g_raw[:, g, :, n0 : n0 + 256].rearrange("p t (c i) -> p c t i", i=4)
-            if g >= 0:
+            if g == 0:
                 nc.vector.tensor_scalar(out=dst, in0=src, scalar1=-1.0, scalar2=None, op0=ALU.mult)
             else:
                 nc.scalar.mul(out=dst, in_=src, mul=-1.0)
@@ -267,36 +267,42 @@ def tile_lagrangenet_kernel(tc, x, min_x, max_x, W, dof, grad_out, out):
             folds(*bounds(gi))
             planes(gi)
 
+        def quarter(qd):
+            regroup(0, qd)
+            quantise_g(0, qd)
+            quantise_g(1, qd)
+
         start_group(0)
         start_group(1)
         finish_leaves(0)
-        produce(0)
         for qd in range(4):
-            regroup(0, qd)
             regroup(1, qd)
-            quantise_g(0, qd)
-            quantise_g(1, qd)
-            if qd == 0:
-                finish_leaves(1)
-            group_of(0, 2 * qd)
-            group_of(0, 2 * qd + 1)
-        start_group(2)
+        produce(0)
+        quarter(0)
+        group_of(0, 0)
+        group_of(0, 1)
+        finish_leaves(1)
+        quarter(1)
+        group_of(0, 2)
+        group_of(0, 3)
         produce(1)
-        finish_leaves(2)
-        start_group(3)
-        produce(2)
-        for nt in range(8):
+        for nt in range(4):
             group_of(1, nt)
-        finish_leaves(3)
-        for fo in range(2, 7):
-            produce(fo + 1)
+        start_group(2)
+        for qd in (2, 3):
+            quarter(qd)
+            for fo in (0, 1):
+                group_of(fo, 2 * qd)
+                group_of(fo, 2 * qd + 1)
+        finish_leaves(2)
+        produce(2)
+        start_group(3)
+        for fo in range(2, 8):
+            if fo + 1 < 8:
+                if fo + 1 in (4, 6):
+                    finish_leaves(fo // 2 + 2)
+                produce(fo + 1)
+                if fo + 1 == 4:
+                    start_group(4)
             for nt in range(8):
                 group_of(fo, nt)
-        accs = []
-        for nt in range(8):
-            acc = psum.tile([P, 512], F32, name="acc")
-            accs.append(acc)
-            one_pass(acc, 7, nt, 0)
-        for nt in range(8):
-            one_pass(accs[nt], 7, nt, 1)
-            drain(accs[nt], 7, nt)

from contextlib import ExitStack

import concourse.mybir as mybir

F32 = mybir.dt.float32
BF16 = mybir.dt.bfloat16
U32 = mybir.dt.uint32
U8 = mybir.dt.uint8
E4X4 = mybir.dt.float8_e4m3fn_x4
E5X4 = mybir.dt.float8_e5m2_x4
ALU = mybir.AluOpType
ACT = mybir.ActivationFunctionType

P = 128
B, F, DOF, N_CLS = 1024, 64, 64, 1024
K = F * DOF
FLOPS = 2 * B * N_CLS * K
BYTES = 4 * N_CLS * K + 2 * B * N_CLS + 2 * B * F + 4

GROUPS = ((0,), (1,), (2, 3), (4, 5), (6, 7))
VECTOR_BANKS = {6: (1, 3, 5, 7), 7: (1, 3, 5, 7)}
PINNED = False


def tile_lagrangenet_kernel(tc, x, min_x, max_x, W, dof, grad_out, out):
    nc = tc.nc
    assert dof == DOF
    with ExitStack() as ctx:
        keep = ctx.enter_context(tc.tile_pool(name="keep", bufs=1))
        embp = ctx.enter_context(tc.tile_pool(name="embp", bufs=2))
        codep = ctx.enter_context(tc.tile_pool(name="codep", bufs=4))
        stagep = ctx.enter_context(tc.tile_pool(name="stagep", bufs=10))
        psum = ctx.enter_context(tc.psum_pool(name="acc", bufs=8))
        if PINNED:
            ctx.enter_context(tc.manual_schedule())

        m_bf = keep.tile([P, 1], BF16, name="m_bf")
        big_bf = keep.tile([P, 1], BF16, name="big_bf")
        x_sb = keep.tile([P, 2, 4, F], BF16, name="x_sb")
        g_raw = keep.tile([P, 2, 4, N_CLS], BF16, name="g_raw")
        nc.sync.dma_start(out=m_bf[:], in_=min_x.partition_broadcast(P))
        nc.sync.dma_start(out=big_bf[:], in_=max_x.partition_broadcast(P))
        nc.sync.dma_start(out=x_sb[:], in_=x.rearrange("(g p t) f -> p g t f", g=2, p=P, t=4))
        for g in range(2):
            nc.sync.dma_start(
                out=g_raw[:, g],
                in_=grad_out[g * 512 : (g + 1) * 512, :].rearrange("(p j) n -> p j n", j=4),
            )

        tab0 = keep.tile([P, 19], F32, name="tab0")
        consts = [-(8.0 * a + 3.5) for a in range(8)] + [-31.5, -16.0, -8.0] + [-(c + 0.5) for c in range(8)]
        for j, v in enumerate(consts):
            nc.vector.memset(tab0[:, j : j + 1], v)
        warm = keep.tile([P, 1], F32, name="warm")
        nc.scalar.activation(out=warm[:], in_=tab0[:, 0:1], func=ACT.Abs)

        big_f = keep.tile([P, 1], F32, name="big_f")
        neg_m = keep.tile([P, 1], F32, name="neg_m")
        n63m = keep.tile([P, 1], F32, name="n63m")
        rng = keep.tile([P, 1], F32, name="rng")
        tab_a = keep.tile([P, 8], F32, name="tab_a")
        tab_y = keep.tile([P, 8], F32, name="tab_y")
        rinv = keep.tile([P, 1], F32, name="rinv")
        c63 = keep.tile([P, 1], F32, name="c63")
        mc = keep.tile([P, 1], F32, name="mc")
        bias1 = keep.tile([P, 1], F32, name="bias1")
        neg_2r = keep.tile([P, 1], F32, name="neg_2r")
        top_x = keep.tile([P, 1], F32, name="top_x")
        nc.vector.tensor_sub(out=rng[:], in0=big_bf[:], in1=m_bf[:])
        nc.vector.reciprocal(out=rinv[:], in_=rng[:])
        nc.vector.tensor_scalar_mul(out=n63m[:], in0=m_bf[:], scalar1=-63.0)
        nc.vector.tensor_scalar_mul(out=c63[:], in0=rinv[:], scalar1=63.0)
        nc.vector.tensor_scalar_mul(out=neg_2r[:], in0=rng[:], scalar1=-2.0)
        nc.vector.tensor_mul(out=mc[:], in0=m_bf[:], in1=c63[:])
        nc.vector.tensor_scalar(
            out=tab_a[:], in0=tab0[:, 0:8], scalar1=rng[:, 0:1], scalar2=n63m[:, 0:1], op0=ALU.mult, op1=ALU.add
        )
        nc.vector.tensor_sub(out=bias1[:], in0=tab0[:, 8:9], in1=mc[:])
        nc.vector.tensor_copy(out=big_f[:], in_=big_bf[:])
        nc.vector.tensor_scalar(out=tab_y[:], in0=tab0[:, 11:19], scalar1=rng[:, 0:1], scalar2=None, op0=ALU.mult)
        nc.vector.tensor_scalar_mul(out=neg_m[:], in0=m_bf[:], scalar1=-1.0)
        nc.vector.scalar_tensor_tensor(
            out=top_x[:], in0=rng[:], scalar=3.5, in1=big_f[:], op0=ALU.mult, op1=ALU.add
        )

        xf = keep.tile([P, 2, F, 4], F32, name="xf")
        above = keep.tile([P, 2, F, 4], F32, name="above")
        side = keep.tile([P, 2, F, 4], F32, name="side")
        xe = keep.tile([P, 2, F, 4], F32, name="xe")
        fold1 = keep.tile([P, 2, F, 4], F32, name="fold1")
        fold2 = keep.tile([P, 2, F, 4], F32, name="fold2")
        fold3 = keep.tile([P, 2, F, 4], F32, name="fold3")

        def token_level(f0, f1):
            nc.vector.tensor_copy(out=xf[:, :, f0:f1, :], in_=x_sb[:, :, :, f0:f1].rearrange("p g t f -> p g f t"))
            nc.vector.tensor_scalar(
                out=above[:, :, f0:f1, :], in0=xf[:, :, f0:f1, :], scalar1=big_f[:, 0:1], scalar2=None, op0=ALU.is_gt
            )
            nc.vector.scalar_tensor_tensor(
                out=side[:, :, f0:f1, :],
                in0=xf[:, :, f0:f1, :],
                scalar=m_bf[:, 0:1],
                in1=above[:, :, f0:f1, :],
                op0=ALU.is_lt,
                op1=ALU.subtract,
            )
            nc.vector.scalar_tensor_tensor(
                out=xe[:, :, f0:f1, :],
                in0=side[:, :, f0:f1, :],
                scalar=neg_2r[:, 0:1],
                in1=xf[:, :, f0:f1, :],
                op0=ALU.mult,
                op1=ALU.add,
            )

        def folds(f0, f1):
            nc.scalar.activation(
                out=fold1[:, :, f0:f1, :], in_=xf[:, :, f0:f1, :], func=ACT.Abs, bias=bias1[:, 0:1], scale=c63[:, 0:1]
            )
            nc.scalar.activation(
                out=fold2[:, :, f0:f1, :], in_=fold1[:, :, f0:f1, :], func=ACT.Abs, bias=tab0[:, 9:10], scale=1.0
            )
            nc.scalar.activation(
                out=fold3[:, :, f0:f1, :], in_=fold2[:, :, f0:f1, :], func=ACT.Abs, bias=tab0[:, 10:11], scale=1.0
            )

        leaves = {}

        def plane_jobs(gi):
            grp = GROUPS[gi]
            nfo = len(grp)
            f0 = 8 * grp[0]
            f1 = f0 + 8 * nfo
            abs_x = keep.tile([P, 2, nfo, 8, 32], F32, name="abs_x%d" % gi)
            abs_y = keep.tile([P, 2, nfo, 8, 32], F32, name="abs_y%d" % gi)
            leaves[gi] = (abs_x, abs_y)

            def x_plane(a):
                nc.scalar.activation(
                    out=abs_x[:, :, :, a, :],
                    in_=xe[:, :, f0:f1, :].rearrange("p g (o l) t -> p g o (l t)", o=nfo),
                    func=ACT.Abs,
                    bias=tab_a[:, a : a + 1],
                    scale=63.0,
                )

            def y_plane(c):
                nc.scalar.activation(
                    out=abs_y[:, :, :, c, :],
                    in_=fold3[:, :, f0:f1, :].rearrange("p g (o l) t -> p g o (l t)", o=nfo),
                    func=ACT.Abs,
                    bias=tab_y[:, c : c + 1],
                    scale=rng[:, 0:1],
                )

            return [(x_plane, a) for a in range(8)] + [(y_plane, c) for c in range(8)]

        def planes(gi):
            for job, k in plane_jobs(gi):
                job(k)

        def finish_leaves(gi):
            nfo = len(GROUPS[gi])
            abs_x, abs_y = leaves[gi]
            row = keep.tile([P, 2, nfo, 8, 32], BF16, name="row%d" % gi)
            col2 = keep.tile([P, 2, nfo, 2, 8, 32], BF16, name="col2%d" % gi)
            nc.vector.tensor_scalar(
                out=col2[:, :, :, 1, :, :],
                in0=abs_y[:],
                scalar1=big_f[:, 0:1],
                scalar2=neg_m[:, 0:1],
                op0=ALU.subtract,
                op1=ALU.min,
            )
            nc.vector.tensor_scalar(
                out=row[:], in0=abs_x[:], scalar1=top_x[:, 0:1], scalar2=neg_m[:, 0:1], op0=ALU.subtract, op1=ALU.min
            )
            for c in range(8):
                if gi >= 0:
                    nc.vector.tensor_copy(out=col2[:, :, :, 0, 7 - c, :], in_=col2[:, :, :, 1, c, :])
                else:
                    nc.scalar.copy(out=col2[:, :, :, 0, 7 - c, :], in_=col2[:, :, :, 1, c, :])
            leaves[gi] = (row, col2)

        g_grp = keep.tile([P, 2, N_CLS, 4], BF16, name="g_grp", align_bytes=64)
        g_codes = keep.tile([P, 2, N_CLS], U32, name="g_codes", align_bytes=64)
        g_scales = keep.tile([P, 2, N_CLS], U8, name="g_scales", align_bytes=64)

        def regroup(g, qd):
            n0 = 256 * qd
            dst = g_grp[:, g, n0 : n0 + 256, :].rearrange("p (c i) t -> p c t i", i=4)
            src = g_raw[:, g, :, n0 : n0 + 256].rearrange("p t (c i) -> p c t i", i=4)
            if g == 0:
                nc.vector.tensor_scalar(out=dst, in0=src, scalar1=-1.0, scalar2=None, op0=ALU.mult)
            else:
                nc.scalar.mul(out=dst, in_=src, mul=-1.0)

        def quantise_g(g, qd):
            n0 = 256 * qd
            nc.vector.quantize_mx(
                out=g_codes[:, g, n0 : n0 + 256].bitcast(E5X4),
                scales=g_scales[:, g, n0 : n0 + 256],
                in_=g_grp[:, g, n0 : n0 + 256, :].rearrange("p n j -> p (n j)"),
            )

        emb_codes = {}

        def produce(fo):
            gi = [i for i, grp in enumerate(GROUPS) if fo in grp][0]
            j = fo - GROUPS[gi][0]
            row, col2 = leaves[gi]
            emb = embp.tile([P, 2, 2048], BF16, name="emb", align_bytes=64)
            codes = codep.tile([P, 2, 512], U32, name="codes", align_bytes=64)
            scales = codep.tile([P, 2, 512], U8, name="scales", align_bytes=64)
            shape = [P, 4, 2, 8, 32]
            for g in range(2):
                nc.vector.tensor_tensor(
                    out=emb[:, g, :].rearrange("p (h r c x) -> p h r c x", h=4, r=2, c=8, x=32),
                    in0=row[:, g, j].rearrange("p (h r) x -> p h r x", h=4, r=2).unsqueeze(3).to_broadcast(shape),
                    in1=col2[:, g, j].unsqueeze(1).to_broadcast(shape),
                    op=ALU.max,
                )
            for g in range(2):
                nc.vector.quantize_mx(out=codes[:, g, :].bitcast(E4X4), scales=scales[:, g, :], in_=emb[:, g, :])
            emb_codes[fo] = (codes, scales)

        def one_pass(acc, fo, nt, g):
            codes, scales = emb_codes[fo]
            nc.tensor.matmul_mx(
                out=acc[:],
                lhsT=g_codes[:, g, nt * P : (nt + 1) * P].bitcast(E5X4),
                lhsT_scale=g_scales[:, g, nt * P : (nt + 1) * P],
                rhs=codes[:, g, :].bitcast(E4X4),
                rhs_scale=scales[:, g, :],
                start=(g == 0),
                stop=(g == 1),
            )

        late_jobs = []
        cursor = [0]

        def drain(acc, fo, nt):
            stage = stagep.tile([P, 512], F32, name="stage")
            src = acc[:].rearrange("p (k l) -> p l k", l=8)
            dst = stage[:].rearrange("p (l k) -> p l k", l=8)
            if nt in VECTOR_BANKS.get(fo, ()):
                nc.vector.tensor_copy(out=dst, in_=src)
            else:
                nc.scalar.copy(out=dst, in_=src)
                if cursor[0] < len(late_jobs):
                    job, k = late_jobs[cursor[0]]
                    cursor[0] += 1
                    job(k)
            nc.sync.dma_start(out=out[nt * P : (nt + 1) * P, fo * 512 : (fo + 1) * 512], in_=stage[:])

        def group_of(fo, nt):
            acc = psum.tile([P, 512], F32, name="acc")
            one_pass(acc, fo, nt, 0)
            one_pass(acc, fo, nt, 1)
            drain(acc, fo, nt)

        def bounds(gi):
            return 8 * GROUPS[gi][0], 8 * GROUPS[gi][-1] + 8

        def start_group(gi):
            token_level(*bounds(gi))
            folds(*bounds(gi))
            planes(gi)

        def quarter(qd):
            regroup(0, qd)
            quantise_g(0, qd)
            quantise_g(1, qd)

        start_group(0)
        start_group(1)
        finish_leaves(0)
        for qd in range(4):
            regroup(1, qd)
        produce(0)
        quarter(0)
        group_of(0, 0)
        group_of(0, 1)
        finish_leaves(1)
        quarter(1)
        group_of(0, 2)
        group_of(0, 3)
        produce(1)
        for nt in range(4):
            group_of(1, nt)
        start_group(2)
        for qd in (2, 3):
            quarter(qd)
            for fo in (0, 1):
                group_of(fo, 2 * qd)
                group_of(fo, 2 * qd + 1)
        finish_leaves(2)
        produce(2)
        start_group(3)
        for fo in range(2, 8):
            if fo + 1 < 8:
                if fo + 1 in (4, 6):
                    finish_leaves(fo // 2 + 2)
                produce(fo + 1)
                if fo + 1 == 4:
                    start_group(4)
            for nt in range(8):
                group_of(fo, nt)
